import numpy as np
import ml_dtypes


def mxq(x, axis, fmt="e4m3"):
    dtype, down = {"e4m3": (ml_dtypes.float8_e4m3fn, 7), "e5m2": (ml_dtypes.float8_e5m2, 14)}[fmt]
    v = np.moveaxis(np.asarray(x, np.float32).astype(ml_dtypes.bfloat16).astype(np.float64), axis, -1)
    blocks = v.reshape(v.shape[:-1] + (-1, 32))
    amax = np.abs(blocks).max(-1, keepdims=True)
    byte = np.maximum(np.where(amax > 0, np.frexp(amax)[1] - 1 + 127, 0) - down, 1)
    scale = np.exp2(byte - 127.0)
    codes = (blocks / scale).astype(np.float32).astype(dtype).astype(np.float64)
    return np.moveaxis((codes * scale).reshape(v.shape), -1, axis)


WIDE = False


def mx_kscale(k):
    if not WIDE:
        return np.ones(k)
    levels = np.array([10, -10, 5, -5, 0])
    a = np.random.permutation(np.resize(levels, k // 512 * 4)).reshape(k // 512, 4)
    idx = np.arange(k)
    return np.exp2(a[idx // 512, idx % 128 // 32])


BF16 = ml_dtypes.bfloat16


def bf(x):
    return np.asarray(x, np.float32).astype(BF16)


def f64(x):
    return np.asarray(x).astype(np.float64)


B, I, H, G = 8192, 256, 256, 4
K = I + H


def sigmoid(v):
    return 1.0 / (1.0 + np.exp(-v))


def hardtanh(v):
    return np.clip(v, -1.0, 1.0)


def setup_inputs():
    s = mx_kscale(K)
    return {"x": bf(np.random.standard_normal((B, I)) * s[:I]),
            "state": bf(np.random.standard_normal((B, H)) * s[I:]),
            "cell": bf(np.random.standard_normal((B, H))),
            "W_in": bf(np.random.standard_normal((G, H, I)) / np.sqrt(K) / s[:I]),
            "W_h": bf(np.random.standard_normal((G, H, H)) / np.sqrt(K) / s[I:])}


def reference(x, state, cell, W_in, W_h):
    z = np.concatenate([f64(x), f64(state)], axis=1)
    W = np.concatenate([f64(W_in), f64(W_h)], axis=2)
    g = mxq(z, 1, "e4m3") @ mxq(W, 2, "e4m3").reshape(G * H, K).T
    g = g.reshape(B, G, H).transpose(1, 0, 2)
    f = sigmoid(g[0])
    i = sigmoid(g[1])
    o = sigmoid(g[2])
    u = hardtanh(g[3])
    new_cell = f * f64(cell) + i * u
    new_state = o * hardtanh(new_cell)
    return (new_state, new_cell)

@@ -1,0 +1,248 @@
+from contextlib import ExitStack
+
+import concourse.mybir as mybir
+from concourse.masks import make_identity
+
+F32 = mybir.dt.float32
+BF16 = mybir.dt.bfloat16
+U32 = mybir.dt.uint32
+U8 = mybir.dt.uint8
+FP8X4 = mybir.dt.float8_e4m3fn_x4
+ALU = mybir.AluOpType
+ACTF = mybir.ActivationFunctionType
+
+P = 128
+B, I, H, G = 8192, 256, 256, 4
+NT = B // P
+NP = NT // 2
+FLOPS = 2 * B * (I + H) * G * H
+
+MANUAL = True
+POOL_COLS = 384
+CELL_PSUM = True
+RELU_A = False
+
+LEAD_T = 4
+LEAD_Q = 2
+LEAD_S = 1
+MARGIN = 8
+
+XCH = [(0, 2), (2, 6)] + [(t, 8) for t in range(8, NT, 8)]
+CCH = [(0, 2), (2, 6)] + [(t, 8) for t in range(8, NT, 8)]
+
+
+def chunk_of(table, t):
+    for ci, (t0, n) in enumerate(table):
+        if t0 <= t < t0 + n:
+            return ci, t - t0
+    raise ValueError("tile outside the table")
+
+
+def tile_lstmhardcell_t_kernel(tc, x, state, cell, W_in, W_h, out_0, out_1):
+    nc = tc.nc
+    with ExitStack() as ctx:
+        const = ctx.enter_context(tc.tile_pool(name="const", bufs=1))
+        inp = ctx.enter_context(tc.tile_pool(name="inp", bufs=1))
+        wpool = ctx.enter_context(tc.tile_pool(name="wpool", bufs=1))
+        zpool = ctx.enter_context(tc.tile_pool(name="zpool", bufs=3))
+        work = ctx.enter_context(tc.tile_pool(name="work", bufs=3))
+        psum = ctx.enter_context(tc.psum_pool(name="psum", bufs=1))
+        if MANUAL:
+            ctx.enter_context(tc.manual_schedule())
+
+        xv = x.rearrange("(p t) k -> p (t k)", t=NT)
+        sv = state.rearrange("(p t) k -> p (t k)", t=NT)
+        cv = cell.rearrange("(p t) k -> p (t k)", t=NT)
+        o0v = out_0.rearrange("(p t) h -> p (t h)", t=NT)
+        o1v = out_1.rearrange("(p t) h -> p (t h)", t=NT)
+        wiv = W_in.rearrange("n h k -> (n h) k").rearrange("(a p) k -> p a k", p=P)
+        whv = W_h.rearrange("n h k -> (n h) k").rearrange("(a p) k -> p a k", p=P)
+
+        xs, ss, cs = {}, {}, {}
+        win, wh = {}, {}
+
+        def load_z(ci):
+            t0, n = XCH[ci]
+            xs[ci] = inp.tile([P, n * I], BF16, name="x%d" % ci)
+            nc.sync.dma_start(out=xs[ci][:], in_=xv[:, t0 * I:(t0 + n) * I])
+            ss[ci] = inp.tile([P, n * H], BF16, name="s%d" % ci)
+            nc.sync.dma_start(out=ss[ci][:], in_=sv[:, t0 * H:(t0 + n) * H])
+
+        def load_c(ci):
+            t0, n = CCH[ci]
+            cs[ci] = inp.tile([P, n * H], BF16, name="c%d" % ci)
+            nc.sync.dma_start(out=cs[ci][:], in_=cv[:, t0 * H:(t0 + n) * H])
+
+        def load_w(half):
+            win[half] = wpool.tile([P, 4 * I], BF16, name="win%d" % half)
+            nc.sync.dma_start(out=win[half][:].rearrange("p (a k) -> p a k", a=4),
+                              in_=wiv[:, 4 * half:4 * half + 4, :])
+            wh[half] = wpool.tile([P, 4 * H], BF16, name="wh%d" % half)
+            nc.sync.dma_start(out=wh[half][:].rearrange("p (a k) -> p a k", a=4),
+                              in_=whv[:, 4 * half:4 * half + 4, :])
+
+        loads = []
+        for ci, (t0, n) in enumerate(XCH):
+            loads.append((t0 // 2 - LEAD_T, 0, load_z, ci))
+        for ci, (t0, n) in enumerate(CCH):
+            loads.append((t0 // 2 - LEAD_S, 1, load_c, ci))
+        loads = sorted(loads, key=lambda e: (e[0], e[1]))
+        done = [0]
+
+        def emit_loads(s):
+            while done[0] < len(loads) and loads[done[0]][0] - MARGIN <= s:
+                e = loads[done[0]]
+                done[0] += 1
+                e[2](e[3])
+
+        load_w(0)
+        load_w(1)
+        emit_loads(-LEAD_T)
+
+        ident_f = const.tile([P, P], F32, name="ident_f")
+        make_identity(nc, ident_f[:])
+        ident_b = const.tile([P, P], BF16, name="ident_b")
+        make_identity(nc, ident_b[:])
+        warm = const.tile([P, 8], F32, name="warm")
+        nc.vector.memset(warm[:], 0.0)
+        nc.scalar.activation(out=warm[:], in_=warm[:], func=ACTF.Sigmoid)
+
+        TB, GRP, ZC, ZS = {}, {}, {}, {}
+        BK = {}
+        SG = {}
+        CB, US, FC, IU, NCL, T4, NST = {}, {}, {}, {}, {}, {}, {}
+        wc, ws = {}, {}
+        TAGS = ["F", "I", "O", "U"]
+
+        def ok(k):
+            return 0 <= k < NP
+
+        def tr(k):
+            TB[k] = psum.tile([P, 512], F32, name="tb", tag="T", bufs=2)
+            for u, src in enumerate((xs, ss)):
+                for t in range(2):
+                    ci, off = chunk_of(XCH, 2 * k + t)
+                    v = src[ci][:].bitcast(F32)
+                    nc.tensor.transpose(TB[k][:, u * 256 + t * P:u * 256 + (t + 1) * P],
+                                        v[:, off * P:(off + 1) * P], ident_f[:])
+
+        def interleave(eng_copy, dst, bank):
+            eng_copy(out=dst[:].bitcast(F32).rearrange("p (c u) -> p c u", u=2),
+                     in_=bank[:].rearrange("p (u c) -> p c u", u=2))
+
+        def ev(k):
+            GRP[k] = zpool.tile([P, 1024], BF16, name="grp", tag="grp", align_bytes=64)
+            interleave(nc.scalar.copy, GRP[k], TB[k])
+
+        def qz(k, t):
+            if t == 0:
+                ZC[k] = zpool.tile([P, 256], U32, name="zc", tag="zc", bufs=4, align_bytes=64)
+                ZS[k] = zpool.tile([P, 256], U8, name="zs", tag="zs", bufs=4, align_bytes=64)
+            nc.vector.quantize_mx(out=ZC[k][:, t * P:(t + 1) * P].bitcast(FP8X4),
+                                  scales=ZS[k][:, t * P:(t + 1) * P],
+                                  in_=GRP[k][:, t * 512:(t + 1) * 512])
+
+        def mx(k, n):
+            BK[(n, k)] = psum.tile([P, 512], F32, name="bk" + TAGS[n], tag=TAGS[n])
+            for t in range(2):
+                nc.tensor.matmul_mx(out=BK[(n, k)][:, t * H:(t + 1) * H],
+                                    lhsT=ZC[k][:, t * P:(t + 1) * P].bitcast(FP8X4),
+                                    lhsT_scale=ZS[k][:, t * P:(t + 1) * P],
+                                    rhs=wc[n][:].bitcast(FP8X4),
+                                    rhs_scale=ws[n][:],
+                                    start=True, stop=True)
+
+        def cell_slice(k):
+            ci, off = chunk_of(CCH, 2 * k)
+            return cs[ci][:, off * H:(off + 2) * H]
+
+        def cellmm(k):
+            CB[k] = psum.tile([P, 512], F32, name="cb", tag="C")
+            nc.tensor.matmul(out=CB[k][:], lhsT=ident_b[:], rhs=cell_slice(k), start=True, stop=True)
+
+        def sig(k, n):
+            SG[(n, k)] = work.tile([P, 512], F32, name="sg" + TAGS[n], tag="sg" + TAGS[n])
+            if n == 3:
+                nc.scalar.activation(out=SG[(n, k)][:], in_=BK[(n, k)][:], func=ACTF.Relu, bias=1.0)
+            else:
+                nc.scalar.activation(out=SG[(n, k)][:], in_=BK[(n, k)][:], func=ACTF.Sigmoid)
+
+        def w_prep():
+            wg = {}
+            for n in range(G):
+                wb = psum.tile([P, 512], F32, name="wb", tag=TAGS[n])
+                for u, src in enumerate((win, wh)):
+                    v = src[n // 2][:].bitcast(F32)
+                    for r in range(2):
+                        a = (n % 2) * 2 + r
+                        nc.tensor.transpose(wb[:, u * 256 + r * P:u * 256 + (r + 1) * P],
+                                            v[:, a * P:(a + 1) * P], ident_f[:])
+                wg[n] = wpool.tile([P, 1024], BF16, name="wg%d" % n, align_bytes=64)
+                interleave(nc.scalar.copy if n % 2 == 0 else nc.vector.tensor_copy, wg[n], wb)
+                for m in ([n - 1] if n < G - 1 else [n - 1, n]):
+                    if m >= 0:
+                        wc[m] = wpool.tile([P, 256], U32, name="wc%d" % m, align_bytes=64)
+                        ws[m] = wpool.tile([P, 256], U8, name="ws%d" % m, align_bytes=64)
+                        nc.vector.quantize_mx(out=wc[m][:].bitcast(FP8X4), scales=ws[m][:], in_=wg[m][:])
+
+        def state_rest(k, c0):
+            if c0 < 512:
+                nc.vector.tensor_tensor(out=NST[k][:, c0:], in0=SG[(2, k)][:, c0:], in1=T4[k][:, c0:],
+                                        op=ALU.mult)
+            nc.sync.dma_start(out=o0v[:, 2 * k * H:(2 * k + 2) * H], in_=NST[k][:])
+
+        w_prep()
+        for s in range(-LEAD_T, NP):
+            emit_loads(s)
+            live = ok(s)
+            if live:
+                US[s] = work.tile([P, 512], F32, name="us", tag="us", bufs=2)
+                if RELU_A:
+                    nc.vector.tensor_scalar(out=US[s][:], in0=SG[(3, s)][:], scalar1=2.0, scalar2=-1.0,
+                                            op0=ALU.min, op1=ALU.add)
+                else:
+                    nc.vector.tensor_scalar(out=US[s][:], in0=BK[(3, s)][:], scalar1=-1.0, scalar2=1.0,
+                                            op0=ALU.max, op1=ALU.min)
+                FC[s] = work.tile([P, 512], F32, name="fc", tag="fc", bufs=2)
+                nc.vector.tensor_tensor(out=FC[s][:], in0=SG[(0, s)][:],
+                                        in1=CB[s][:] if CELL_PSUM else cell_slice(s), op=ALU.mult)
+                IU[s] = work.tile([P, 512], F32, name="iu", tag="iu", bufs=2)
+                nc.vector.tensor_tensor(out=IU[s][:], in0=SG[(1, s)][:], in1=US[s][:], op=ALU.mult)
+                if s > 0:
+                    state_rest(s - 1, POOL_COLS)
+            if ok(s + LEAD_Q):
+                qz(s + LEAD_Q, 0)
+            if live:
+                NCL[s] = work.tile([P, 512], F32, name="ncl", tag="ncl", bufs=4)
+                nc.vector.tensor_tensor(out=NCL[s][:], in0=FC[s][:], in1=IU[s][:], op=ALU.add)
+                nc.sync.dma_start(out=o1v[:, 2 * s * H:(2 * s + 2) * H], in_=NCL[s][:])
+            if ok(s + LEAD_Q):
+                qz(s + LEAD_Q, 1)
+            if live:
+                T4[s] = work.tile([P, 512], F32, name="t4", tag="t4")
+                nc.vector.tensor_scalar(out=T4[s][:], in0=NCL[s][:], scalar1=-1.0, scalar2=1.0,
+                                        op0=ALU.max, op1=ALU.min)
+                NST[s] = work.tile([P, 512], F32, name="nst", tag="nst", bufs=4)
+                if s == NP - 1:
+                    state_rest(s, 0)
+                elif POOL_COLS > 0:
+                    pc = POOL_COLS
+                    nc.gpsimd.tensor_tensor(out=NST[s][:, :pc], in0=SG[(2, s)][:, :pc], in1=T4[s][:, :pc],
+                                            op=ALU.mult)
+            k = s + LEAD_S
+            if ok(k):
+                mx(k, 3)
+                if CELL_PSUM:
+                    cellmm(k)
+                for n in range(3):
+                    mx(k, n)
+            if ok(s + LEAD_T):
+                tr(s + LEAD_T)
+            if ok(k):
+                sig(k, 0)
+                if RELU_A:
+                    sig(k, 3)
+                sig(k, 1)
+                sig(k, 2)
+            if ok(s + LEAD_T):
+                ev(s + LEAD_T)

@@ -18,9 +18,9 @@ NP = NT // 2
 FLOPS = 2 * B * (I + H) * G * H
 
 MANUAL = True
-POOL_COLS = 384
-CELL_PSUM = True
-RELU_A = False
+POOL_COLS = 0
+CELL_PSUM = False
+RELU_A = True
 
 LEAD_T = 4
 LEAD_Q = 2

@@ -18,24 +18,29 @@ NP = NT // 2
 FLOPS = 2 * B * (I + H) * G * H
 
 MANUAL = True
-POOL_COLS = 0
-CELL_PSUM = False
-RELU_A = True
-
-LEAD_T = 4
-LEAD_Q = 2
-LEAD_S = 1
+LEAD_T = 6
+LEAD_S = 3
 MARGIN = 8
 
-XCH = [(0, 2), (2, 6)] + [(t, 8) for t in range(8, NT, 8)]
-CCH = [(0, 2), (2, 6)] + [(t, 8) for t in range(8, NT, 8)]
+GROUPS = [(0, 1), (1, 1)] + [(k, 2) for k in range(2, NP - 2, 2)] + [(NP - 2, 1), (NP - 1, 1)]
+NG = len(GROUPS)
+XCH = [(0, 4), (4, 4)] + [(t, 8) for t in range(8, NT, 8)]
+FG, IG, OG, UG = 0, 1, 2, 3
+TAGS = ["F", "I", "O", "U"]
 
 
-def chunk_of(table, t):
-    for ci, (t0, n) in enumerate(table):
+def chunk_of(t):
+    for ci, (t0, n) in enumerate(XCH):
         if t0 <= t < t0 + n:
             return ci, t - t0
     raise ValueError("tile outside the table")
+
+
+def group_of(k):
+    for g, (k0, n) in enumerate(GROUPS):
+        if k0 <= k < k0 + n:
+            return g, k - k0
+    raise ValueError("pair outside the table")
 
 
 def tile_lstmhardcell_t_kernel(tc, x, state, cell, W_in, W_h, out_0, out_1):
@@ -44,8 +49,8 @@ def tile_lstmhardcell_t_kernel(tc, x, state, cell, W_in, W_h, out_0, out_1):
         const = ctx.enter_context(tc.tile_pool(name="const", bufs=1))
         inp = ctx.enter_context(tc.tile_pool(name="inp", bufs=1))
         wpool = ctx.enter_context(tc.tile_pool(name="wpool", bufs=1))
-        zpool = ctx.enter_context(tc.tile_pool(name="zpool", bufs=3))
-        work = ctx.enter_context(tc.tile_pool(name="work", bufs=3))
+        zpool = ctx.enter_context(tc.tile_pool(name="zpool", bufs=4))
+        work = ctx.enter_context(tc.tile_pool(name="work", bufs=2))
         psum = ctx.enter_context(tc.psum_pool(name="psum", bufs=1))
         if MANUAL:
             ctx.enter_context(tc.manual_schedule())
@@ -69,7 +74,7 @@ def tile_lstmhardcell_t_kernel(tc, x, state, cell, W_in, W_h, out_0, out_1):
             nc.sync.dma_start(out=ss[ci][:], in_=sv[:, t0 * H:(t0 + n) * H])
 
         def load_c(ci):
-            t0, n = CCH[ci]
+            t0, n = XCH[ci]
             cs[ci] = inp.tile([P, n * H], BF16, name="c%d" % ci)
             nc.sync.dma_start(out=cs[ci][:], in_=cv[:, t0 * H:(t0 + n) * H])
 
@@ -84,8 +89,7 @@ def tile_lstmhardcell_t_kernel(tc, x, state, cell, W_in, W_h, out_0, out_1):
         loads = []
         for ci, (t0, n) in enumerate(XCH):
             loads.append((t0 // 2 - LEAD_T, 0, load_z, ci))
-        for ci, (t0, n) in enumerate(CCH):
-            loads.append((t0 // 2 - LEAD_S, 1, load_c, ci))
+            loads.append((t0 // 2, 1, load_c, ci))
         loads = sorted(loads, key=lambda e: (e[0], e[1]))
         done = [0]
 
@@ -101,18 +105,16 @@ def tile_lstmhardcell_t_kernel(tc, x, state, cell, W_in, W_h, out_0, out_1):
 
         ident_f = const.tile([P, P], F32, name="ident_f")
         make_identity(nc, ident_f[:])
-        ident_b = const.tile([P, P], BF16, name="ident_b")
-        make_identity(nc, ident_b[:])
         warm = const.tile([P, 8], F32, name="warm")
         nc.vector.memset(warm[:], 0.0)
         nc.scalar.activation(out=warm[:], in_=warm[:], func=ACTF.Sigmoid)
 
-        TB, GRP, ZC, ZS = {}, {}, {}, {}
-        BK = {}
+        TB, GRP, ZC, ZS, BK = {}, {}, {}, {}, {}
         SG = {}
-        CB, US, FC, IU, NCL, T4, NST = {}, {}, {}, {}, {}, {}, {}
+        US, T4 = {}, {}
         wc, ws = {}, {}
-        TAGS = ["F", "I", "O", "U"]
+        copied = set()
+        quantised = set()
 
         def ok(k):
             return 0 <= k < NP
@@ -121,51 +123,52 @@ def tile_lstmhardcell_t_kernel(tc, x, state, cell, W_in, W_h, out_0, out_1):
             TB[k] = psum.tile([P, 512], F32, name="tb", tag="T", bufs=2)
             for u, src in enumerate((xs, ss)):
                 for t in range(2):
-                    ci, off = chunk_of(XCH, 2 * k + t)
+                    ci, off = chunk_of(2 * k + t)
                     v = src[ci][:].bitcast(F32)
                     nc.tensor.transpose(TB[k][:, u * 256 + t * P:u * 256 + (t + 1) * P],
                                         v[:, off * P:(off + 1) * P], ident_f[:])
 
-        def interleave(eng_copy, dst, bank):
-            eng_copy(out=dst[:].bitcast(F32).rearrange("p (c u) -> p c u", u=2),
+        def interleave(eng_copy, dst_f32, bank):
+            eng_copy(out=dst_f32.rearrange("p (c u) -> p c u", u=2),
                      in_=bank[:].rearrange("p (u c) -> p c u", u=2))
 
         def ev(k):
-            GRP[k] = zpool.tile([P, 1024], BF16, name="grp", tag="grp", align_bytes=64)
-            interleave(nc.scalar.copy, GRP[k], TB[k])
+            g, pos = group_of(k)
+            if pos == 0:
+                GRP[g] = zpool.tile([P, 2048], BF16, name="grp", tag="grp", align_bytes=64)
+            interleave(nc.scalar.copy, GRP[g][:].bitcast(F32)[:, pos * 512:(pos + 1) * 512], TB[k])
+            copied.add(k)
 
-        def qz(k, t):
-            if t == 0:
-                ZC[k] = zpool.tile([P, 256], U32, name="zc", tag="zc", bufs=4, align_bytes=64)
-                ZS[k] = zpool.tile([P, 256], U8, name="zs", tag="zs", bufs=4, align_bytes=64)
-            nc.vector.quantize_mx(out=ZC[k][:, t * P:(t + 1) * P].bitcast(FP8X4),
-                                  scales=ZS[k][:, t * P:(t + 1) * P],
-                                  in_=GRP[k][:, t * 512:(t + 1) * 512])
+        def qz(g):
+            n = GROUPS[g][1]
+            ZC[g] = zpool.tile([P, 512], U32, name="zc", tag="zc", align_bytes=64)
+            ZS[g] = zpool.tile([P, 512], U8, name="zs", tag="zs", align_bytes=64)
+            nc.vector.quantize_mx(out=ZC[g][:, :n * 256].bitcast(FP8X4), scales=ZS[g][:, :n * 256],
+                                  in_=GRP[g][:, :n * 1024])
+            quantised.add(g)
 
         def mx(k, n):
+            g, pos = group_of(k)
             BK[(n, k)] = psum.tile([P, 512], F32, name="bk" + TAGS[n], tag=TAGS[n])
             for t in range(2):
+                c0 = (2 * pos + t) * P
                 nc.tensor.matmul_mx(out=BK[(n, k)][:, t * H:(t + 1) * H],
-                                    lhsT=ZC[k][:, t * P:(t + 1) * P].bitcast(FP8X4),
-                                    lhsT_scale=ZS[k][:, t * P:(t + 1) * P],
+                                    lhsT=ZC[g][:, c0:c0 + P].bitcast(FP8X4),
+                                    lhsT_scale=ZS[g][:, c0:c0 + P],
                                     rhs=wc[n][:].bitcast(FP8X4),
                                     rhs_scale=ws[n][:],
                                     start=True, stop=True)
 
-        def cell_slice(k):
-            ci, off = chunk_of(CCH, 2 * k)
-            return cs[ci][:, off * H:(off + 2) * H]
-
-        def cellmm(k):
-            CB[k] = psum.tile([P, 512], F32, name="cb", tag="C")
-            nc.tensor.matmul(out=CB[k][:], lhsT=ident_b[:], rhs=cell_slice(k), start=True, stop=True)
-
-        def sig(k, n):
-            SG[(n, k)] = work.tile([P, 512], F32, name="sg" + TAGS[n], tag="sg" + TAGS[n])
-            if n == 3:
-                nc.scalar.activation(out=SG[(n, k)][:], in_=BK[(n, k)][:], func=ACTF.Relu, bias=1.0)
+        def act(k, n):
+            g, pos = group_of(k)
+            if pos == 0:
+                SG[(n, g)] = work.tile([P, 1024], F32, name="sg" + TAGS[n], tag="sg" + TAGS[n],
+                                       bufs=4 if n in (FG, OG) else 3)
+            dst = SG[(n, g)][:, pos * 512:(pos + 1) * 512]
+            if n == UG:
+                nc.scalar.activation(out=dst, in_=BK[(n, k)][:], func=ACTF.Relu, bias=1.0)
             else:
-                nc.scalar.activation(out=SG[(n, k)][:], in_=BK[(n, k)][:], func=ACTF.Sigmoid)
+                nc.scalar.activation(out=dst, in_=BK[(n, k)][:], func=ACTF.Sigmoid)
 
         def w_prep():
             wg = {}
@@ -178,71 +181,86 @@ def tile_lstmhardcell_t_kernel(tc, x, state, cell, W_in, W_h, out_0, out_1):
                         nc.tensor.transpose(wb[:, u * 256 + r * P:u * 256 + (r + 1) * P],
                                             v[:, a * P:(a + 1) * P], ident_f[:])
                 wg[n] = wpool.tile([P, 1024], BF16, name="wg%d" % n, align_bytes=64)
-                interleave(nc.scalar.copy if n % 2 == 0 else nc.vector.tensor_copy, wg[n], wb)
+                interleave(nc.scalar.copy if n % 2 == 0 else nc.vector.tensor_copy,
+                           wg[n][:].bitcast(F32), wb)
                 for m in ([n - 1] if n < G - 1 else [n - 1, n]):
                     if m >= 0:
                         wc[m] = wpool.tile([P, 256], U32, name="wc%d" % m, align_bytes=64)
                         ws[m] = wpool.tile([P, 256], U8, name="ws%d" % m, align_bytes=64)
                         nc.vector.quantize_mx(out=wc[m][:].bitcast(FP8X4), scales=ws[m][:], in_=wg[m][:])
 
-        def state_rest(k, c0):
-            if c0 < 512:
-                nc.vector.tensor_tensor(out=NST[k][:, c0:], in0=SG[(2, k)][:, c0:], in1=T4[k][:, c0:],
-                                        op=ALU.mult)
-            nc.sync.dma_start(out=o0v[:, 2 * k * H:(2 * k + 2) * H], in_=NST[k][:])
+        def cols(g):
+            return GROUPS[g][1] * 512
+
+        def dram_cols(g):
+            k0, n = GROUPS[g]
+            return slice(2 * k0 * H, 2 * (k0 + n) * H)
+
+        def clip_u(g):
+            w = cols(g)
+            US[g] = work.tile([P, 1024], F32, name="us", tag="us")
+            nc.vector.tensor_scalar(out=US[g][:, :w], in0=SG[(UG, g)][:, :w], scalar1=2.0, scalar2=-1.0,
+                                    op0=ALU.min, op1=ALU.add)
+
+        def f_cell(g):
+            w = cols(g)
+            ci, off = chunk_of(2 * GROUPS[g][0])
+            f = SG[(FG, g)][:, :w]
+            nc.vector.tensor_tensor(out=f, in0=f, in1=cs[ci][:, off * H:off * H + w], op=ALU.mult)
+
+        def i_u(g):
+            w = cols(g)
+            nc.vector.tensor_tensor(out=US[g][:, :w], in0=SG[(IG, g)][:, :w], in1=US[g][:, :w], op=ALU.mult)
+
+        def new_cell(g):
+            w = cols(g)
+            f = SG[(FG, g)][:, :w]
+            nc.vector.tensor_tensor(out=f, in0=f, in1=US[g][:, :w], op=ALU.add)
+            nc.sync.dma_start(out=o1v[:, dram_cols(g)], in_=f)
+
+        def clip_c(g):
+            w = cols(g)
+            T4[g] = work.tile([P, 1024], F32, name="t4", tag="t4")
+            nc.vector.tensor_scalar(out=T4[g][:, :w], in0=SG[(FG, g)][:, :w], scalar1=-1.0, scalar2=1.0,
+                                    op0=ALU.max, op1=ALU.min)
+
+        def new_state(g):
+            w = cols(g)
+            o = SG[(OG, g)][:, :w]
+            nc.vector.tensor_tensor(out=o, in0=o, in1=T4[g][:, :w], op=ALU.mult)
+            nc.sync.dma_start(out=o0v[:, dram_cols(g)], in_=o)
+
+        def ready(g):
+            k0, n = GROUPS[g]
+            return all((k0 + j) in copied for j in range(n))
 
         w_prep()
         for s in range(-LEAD_T, NP):
             emit_loads(s)
-            live = ok(s)
-            if live:
-                US[s] = work.tile([P, 512], F32, name="us", tag="us", bufs=2)
-                if RELU_A:
-                    nc.vector.tensor_scalar(out=US[s][:], in0=SG[(3, s)][:], scalar1=2.0, scalar2=-1.0,
-                                            op0=ALU.min, op1=ALU.add)
-                else:
-                    nc.vector.tensor_scalar(out=US[s][:], in0=BK[(3, s)][:], scalar1=-1.0, scalar2=1.0,
-                                            op0=ALU.max, op1=ALU.min)
-                FC[s] = work.tile([P, 512], F32, name="fc", tag="fc", bufs=2)
-                nc.vector.tensor_tensor(out=FC[s][:], in0=SG[(0, s)][:],
-                                        in1=CB[s][:] if CELL_PSUM else cell_slice(s), op=ALU.mult)
-                IU[s] = work.tile([P, 512], F32, name="iu", tag="iu", bufs=2)
-                nc.vector.tensor_tensor(out=IU[s][:], in0=SG[(1, s)][:], in1=US[s][:], op=ALU.mult)
-                if s > 0:
-                    state_rest(s - 1, POOL_COLS)
-            if ok(s + LEAD_Q):
-                qz(s + LEAD_Q, 0)
-            if live:
-                NCL[s] = work.tile([P, 512], F32, name="ncl", tag="ncl", bufs=4)
-                nc.vector.tensor_tensor(out=NCL[s][:], in0=FC[s][:], in1=IU[s][:], op=ALU.add)
-                nc.sync.dma_start(out=o1v[:, 2 * s * H:(2 * s + 2) * H], in_=NCL[s][:])
-            if ok(s + LEAD_Q):
-                qz(s + LEAD_Q, 1)
-            if live:
-                T4[s] = work.tile([P, 512], F32, name="t4", tag="t4")
-                nc.vector.tensor_scalar(out=T4[s][:], in0=NCL[s][:], scalar1=-1.0, scalar2=1.0,
-                                        op0=ALU.max, op1=ALU.min)
-                NST[s] = work.tile([P, 512], F32, name="nst", tag="nst", bufs=4)
-                if s == NP - 1:
-                    state_rest(s, 0)
-                elif POOL_COLS > 0:
-                    pc = POOL_COLS
-                    nc.gpsimd.tensor_tensor(out=NST[s][:, :pc], in0=SG[(2, s)][:, :pc], in1=T4[s][:, :pc],
-                                            op=ALU.mult)
+            if ok(s) and group_of(s)[1] == GROUPS[group_of(s)[0]][1] - 1:
+                g = group_of(s)[0]
+                clip_u(g)
+                if g > 0:
+                    clip_c(g - 1)
+                f_cell(g)
+                if g > 0:
+                    new_state(g - 1)
+                i_u(g)
+                if g + 2 < NG and (g + 2) not in quantised and ready(g + 2):
+                    qz(g + 2)
+                new_cell(g)
             k = s + LEAD_S
             if ok(k):
-                mx(k, 3)
-                if CELL_PSUM:
-                    cellmm(k)
-                for n in range(3):
+                if group_of(k)[0] not in quantised:
+                    qz(group_of(k)[0])
+                for n in (UG, FG, IG, OG):
                     mx(k, n)
             if ok(s + LEAD_T):
                 tr(s + LEAD_T)
             if ok(k):
-                sig(k, 0)
-                if RELU_A:
-                    sig(k, 3)
-                sig(k, 1)
-                sig(k, 2)
+                for n in (UG, FG, IG, OG):
+                    act(k, n)
             if ok(s + LEAD_T):
                 ev(s + LEAD_T)
+        clip_c(NG - 1)
+        new_state(NG - 1)

@@ -19,10 +19,13 @@ FLOPS = 2 * B * (I + H) * G * H
 
 MANUAL = True
 LEAD_T = 6
-LEAD_S = 3
+LEAD_S = 2
 MARGIN = 8
+RR_FROM = 6
+RR_EVERY = 3
+D_UNTIL = 4
 
-GROUPS = [(0, 1), (1, 1)] + [(k, 2) for k in range(2, NP - 2, 2)] + [(NP - 2, 1), (NP - 1, 1)]
+GROUPS = [(k, 1) for k in range(4)] + [(k, 2) for k in range(4, NP - 2, 2)] + [(NP - 2, 1), (NP - 1, 1)]
 NG = len(GROUPS)
 XCH = [(0, 4), (4, 4)] + [(t, 8) for t in range(8, NT, 8)]
 FG, IG, OG, UG = 0, 1, 2, 3
@@ -78,19 +81,19 @@ def tile_lstmhardcell_t_kernel(tc, x, state, cell, W_in, W_h, out_0, out_1):
             cs[ci] = inp.tile([P, n * H], BF16, name="c%d" % ci)
             nc.sync.dma_start(out=cs[ci][:], in_=cv[:, t0 * H:(t0 + n) * H])
 
-        def load_w(half):
-            win[half] = wpool.tile([P, 4 * I], BF16, name="win%d" % half)
-            nc.sync.dma_start(out=win[half][:].rearrange("p (a k) -> p a k", a=4),
-                              in_=wiv[:, 4 * half:4 * half + 4, :])
-            wh[half] = wpool.tile([P, 4 * H], BF16, name="wh%d" % half)
-            nc.sync.dma_start(out=wh[half][:].rearrange("p (a k) -> p a k", a=4),
-                              in_=whv[:, 4 * half:4 * half + 4, :])
+        def load_w(n):
+            win[n] = wpool.tile([P, 2 * I], BF16, name="win%d" % n)
+            nc.sync.dma_start(out=win[n][:].rearrange("p (a k) -> p a k", a=2),
+                              in_=wiv[:, 2 * n:2 * n + 2, :])
+            wh[n] = wpool.tile([P, 2 * H], BF16, name="wh%d" % n)
+            nc.sync.dma_start(out=wh[n][:].rearrange("p (a k) -> p a k", a=2),
+                              in_=whv[:, 2 * n:2 * n + 2, :])
 
         loads = []
         for ci, (t0, n) in enumerate(XCH):
             loads.append((t0 // 2 - LEAD_T, 0, load_z, ci))
             loads.append((t0 // 2, 1, load_c, ci))
-        loads = sorted(loads, key=lambda e: (e[0], e[1]))
+        loads = [e for e in sorted(loads, key=lambda e: (e[0], e[1])) if e[3] > 0]
         done = [0]
 
         def emit_loads(s):
@@ -99,8 +102,12 @@ def tile_lstmhardcell_t_kernel(tc, x, state, cell, W_in, W_h, out_0, out_1):
                 done[0] += 1
                 e[2](e[3])
 
-        load_w(0)
-        load_w(1)
+        load_w(FG)
+        load_w(UG)
+        load_z(0)
+        load_w(IG)
+        load_w(OG)
+        load_c(0)
         emit_loads(-LEAD_T)
 
         ident_f = const.tile([P, P], F32, name="ident_f")
@@ -149,7 +156,7 @@ def tile_lstmhardcell_t_kernel(tc, x, state, cell, W_in, W_h, out_0, out_1):
 
         def mx(k, n):
             g, pos = group_of(k)
-            BK[(n, k)] = psum.tile([P, 512], F32, name="bk" + TAGS[n], tag=TAGS[n])
+            BK[(n, k)] = psum.tile([P, 512], F32, name="bk" + TAGS[n], tag=TAGS[n], bufs=2 if n == UG else 1)
             for t in range(2):
                 c0 = (2 * pos + t) * P
                 nc.tensor.matmul_mx(out=BK[(n, k)][:, t * H:(t + 1) * H],
@@ -165,29 +172,31 @@ def tile_lstmhardcell_t_kernel(tc, x, state, cell, W_in, W_h, out_0, out_1):
                 SG[(n, g)] = work.tile([P, 1024], F32, name="sg" + TAGS[n], tag="sg" + TAGS[n],
                                        bufs=4 if n in (FG, OG) else 3)
             dst = SG[(n, g)][:, pos * 512:(pos + 1) * 512]
-            if n == UG:
+            if n == UG and rr(g):
+                nc.scalar.activation(out=dst, in_=BK[(n, k)][:], func=ACTF.Relu, bias=1.0, scale=-1.0)
+                if pos == GROUPS[g][1] - 1:
+                    whole = SG[(n, g)][:, :cols(g)]
+                    nc.scalar.activation(out=whole, in_=whole, func=ACTF.Relu, bias=2.0, scale=-1.0)
+            elif n == UG:
                 nc.scalar.activation(out=dst, in_=BK[(n, k)][:], func=ACTF.Relu, bias=1.0)
             else:
                 nc.scalar.activation(out=dst, in_=BK[(n, k)][:], func=ACTF.Sigmoid)
 
-        def w_prep():
-            wg = {}
-            for n in range(G):
-                wb = psum.tile([P, 512], F32, name="wb", tag=TAGS[n])
-                for u, src in enumerate((win, wh)):
-                    v = src[n // 2][:].bitcast(F32)
-                    for r in range(2):
-                        a = (n % 2) * 2 + r
-                        nc.tensor.transpose(wb[:, u * 256 + r * P:u * 256 + (r + 1) * P],
-                                            v[:, a * P:(a + 1) * P], ident_f[:])
-                wg[n] = wpool.tile([P, 1024], BF16, name="wg%d" % n, align_bytes=64)
-                interleave(nc.scalar.copy if n % 2 == 0 else nc.vector.tensor_copy,
-                           wg[n][:].bitcast(F32), wb)
-                for m in ([n - 1] if n < G - 1 else [n - 1, n]):
-                    if m >= 0:
-                        wc[m] = wpool.tile([P, 256], U32, name="wc%d" % m, align_bytes=64)
-                        ws[m] = wpool.tile([P, 256], U8, name="ws%d" % m, align_bytes=64)
-                        nc.vector.quantize_mx(out=wc[m][:].bitcast(FP8X4), scales=ws[m][:], in_=wg[m][:])
+        def w_gate(n, eng_copy):
+            wb = psum.tile([P, 512], F32, name="wb", tag=TAGS[n], bufs=2 if n == UG else 1)
+            for u, src in enumerate((win, wh)):
+                v = src[n][:].bitcast(F32)
+                for r in range(2):
+                    nc.tensor.transpose(wb[:, u * 256 + r * P:u * 256 + (r + 1) * P],
+                                        v[:, r * P:(r + 1) * P], ident_f[:])
+            wg = wpool.tile([P, 1024], BF16, name="wg%d" % n, align_bytes=64)
+            interleave(eng_copy, wg[:].bitcast(F32), wb)
+            wc[n] = wpool.tile([P, 256], U32, name="wc%d" % n, align_bytes=64)
+            ws[n] = wpool.tile([P, 256], U8, name="ws%d" % n, align_bytes=64)
+            nc.vector.quantize_mx(out=wc[n][:].bitcast(FP8X4), scales=ws[n][:], in_=wg[:])
+
+        def rr(g):
+            return g >= RR_FROM and (g - RR_FROM) % RR_EVERY == 0
 
         def cols(g):
             return GROUPS[g][1] * 512
@@ -199,6 +208,11 @@ def tile_lstmhardcell_t_kernel(tc, x, state, cell, W_in, W_h, out_0, out_1):
         def clip_u(g):
             w = cols(g)
             US[g] = work.tile([P, 1024], F32, name="us", tag="us")
+            if g < D_UNTIL:
+                for j in range(GROUPS[g][1]):
+                    nc.vector.tensor_scalar(out=US[g][:, j * 512:(j + 1) * 512], in0=BK[(UG, GROUPS[g][0] + j)][:],
+                                            scalar1=-1.0, scalar2=1.0, op0=ALU.max, op1=ALU.min)
+                return
             nc.vector.tensor_scalar(out=US[g][:, :w], in0=SG[(UG, g)][:, :w], scalar1=2.0, scalar2=-1.0,
                                     op0=ALU.min, op1=ALU.add)
 
@@ -210,6 +224,11 @@ def tile_lstmhardcell_t_kernel(tc, x, state, cell, W_in, W_h, out_0, out_1):
 
         def i_u(g):
             w = cols(g)
+            if rr(g):
+                US[g] = work.tile([P, 1024], F32, name="us", tag="us")
+                nc.vector.scalar_tensor_tensor(out=US[g][:, :w], in0=SG[(UG, g)][:, :w], scalar=-1.0,
+                                               in1=SG[(IG, g)][:, :w], op0=ALU.add, op1=ALU.mult)
+                return
             nc.vector.tensor_tensor(out=US[g][:, :w], in0=SG[(IG, g)][:, :w], in1=US[g][:, :w], op=ALU.mult)
 
         def new_cell(g):
@@ -234,18 +253,33 @@ def tile_lstmhardcell_t_kernel(tc, x, state, cell, W_in, W_h, out_0, out_1):
             k0, n = GROUPS[g]
             return all((k0 + j) in copied for j in range(n))
 
-        w_prep()
-        for s in range(-LEAD_T, NP):
+        w_gate(FG, nc.scalar.copy)
+        w_gate(UG, nc.scalar.copy)
+        tr(0)
+        ev(0)
+        tr(1)
+        ev(1)
+        qz(0)
+        w_gate(IG, nc.vector.tensor_copy)
+        qz(1)
+        w_gate(OG, nc.vector.tensor_copy)
+        nxt = [2]
+        order = (FG, UG, IG, OG)
+        for s in range(-LEAD_S, NP):
             emit_loads(s)
             if ok(s) and group_of(s)[1] == GROUPS[group_of(s)[0]][1] - 1:
                 g = group_of(s)[0]
-                clip_u(g)
-                if g > 0:
-                    clip_c(g - 1)
                 f_cell(g)
                 if g > 0:
+                    clip_c(g - 1)
+                if not rr(g):
+                    clip_u(g)
+                else:
+                    i_u(g)
+                if g > 0:
                     new_state(g - 1)
-                i_u(g)
+                if not rr(g):
+                    i_u(g)
                 if g + 2 < NG and (g + 2) not in quantised and ready(g + 2):
                     qz(g + 2)
                 new_cell(g)
@@ -253,14 +287,17 @@ def tile_lstmhardcell_t_kernel(tc, x, state, cell, W_in, W_h, out_0, out_1):
             if ok(k):
                 if group_of(k)[0] not in quantised:
                     qz(group_of(k)[0])
-                for n in (UG, FG, IG, OG):
+                for n in order:
                     mx(k, n)
-            if ok(s + LEAD_T):
-                tr(s + LEAD_T)
+            first = nxt[0]
+            while nxt[0] <= min(s + LEAD_T, NP - 1) and nxt[0] - first < 2:
+                tr(nxt[0])
+                nxt[0] += 1
             if ok(k):
-                for n in (UG, FG, IG, OG):
-                    act(k, n)
-            if ok(s + LEAD_T):
-                ev(s + LEAD_T)
+                for n in order:
+                    if n != UG or group_of(k)[0] >= D_UNTIL:
+                        act(k, n)
+            for j in range(first, nxt[0]):
+                ev(j)
         clip_c(NG - 1)
         new_state(NG - 1)

@@ -17,7 +17,7 @@ NT = B // P
 NP = NT // 2
 FLOPS = 2 * B * (I + H) * G * H
 
-MANUAL = True
+MANUAL = False
 LEAD_T = 6
 LEAD_S = 2
 MARGIN = 8

@@ -21,13 +21,12 @@ MANUAL = False
 LEAD_T = 6
 LEAD_S = 2
 MARGIN = 8
-RR_FROM = 6
-RR_EVERY = 3
+RR_SET = (6, 9, 12, 14, 15, 16, 17, 18)
 D_UNTIL = 4
 
 GROUPS = [(k, 1) for k in range(4)] + [(k, 2) for k in range(4, NP - 2, 2)] + [(NP - 2, 1), (NP - 1, 1)]
 NG = len(GROUPS)
-XCH = [(0, 4), (4, 4)] + [(t, 8) for t in range(8, NT, 8)]
+XCH = [(0, 2), (2, 2), (4, 4)] + [(t, 8) for t in range(8, NT, 8)]
 FG, IG, OG, UG = 0, 1, 2, 3
 TAGS = ["F", "I", "O", "U"]
 
@@ -103,11 +102,11 @@ def tile_lstmhardcell_t_kernel(tc, x, state, cell, W_in, W_h, out_0, out_1):
                 e[2](e[3])
 
         load_w(FG)
-        load_w(UG)
         load_z(0)
+        load_w(UG)
+        load_c(0)
         load_w(IG)
         load_w(OG)
-        load_c(0)
         emit_loads(-LEAD_T)
 
         ident_f = const.tile([P, P], F32, name="ident_f")
@@ -196,7 +195,7 @@ def tile_lstmhardcell_t_kernel(tc, x, state, cell, W_in, W_h, out_0, out_1):
             nc.vector.quantize_mx(out=wc[n][:].bitcast(FP8X4), scales=ws[n][:], in_=wg[:])
 
         def rr(g):
-            return g >= RR_FROM and (g - RR_FROM) % RR_EVERY == 0
+            return g in RR_SET
 
         def cols(g):
             return GROUPS[g][1] * 512
@@ -254,16 +253,13 @@ def tile_lstmhardcell_t_kernel(tc, x, state, cell, W_in, W_h, out_0, out_1):
             return all((k0 + j) in copied for j in range(n))
 
         w_gate(FG, nc.scalar.copy)
-        w_gate(UG, nc.scalar.copy)
         tr(0)
         ev(0)
-        tr(1)
-        ev(1)
         qz(0)
+        w_gate(UG, nc.scalar.copy)
         w_gate(IG, nc.vector.tensor_copy)
-        qz(1)
         w_gate(OG, nc.vector.tensor_copy)
-        nxt = [2]
+        nxt = [1]
         order = (FG, UG, IG, OG)
         for s in range(-LEAD_S, NP):
             emit_loads(s)

from contextlib import ExitStack

import concourse.mybir as mybir
from concourse.masks import make_identity

F32 = mybir.dt.float32
BF16 = mybir.dt.bfloat16
U32 = mybir.dt.uint32
U8 = mybir.dt.uint8
FP8X4 = mybir.dt.float8_e4m3fn_x4
ALU = mybir.AluOpType
ACTF = mybir.ActivationFunctionType

P = 128
B, I, H, G = 8192, 256, 256, 4
NT = B // P
NP = NT // 2
FLOPS = 2 * B * (I + H) * G * H

MANUAL = False
LEAD_T = 6
LEAD_S = 2
MARGIN = 8
RR_SET = (6, 9, 12, 14, 15, 16, 17, 18)
D_UNTIL = 4

GROUPS = [(k, 1) for k in range(4)] + [(k, 2) for k in range(4, NP - 2, 2)] + [(NP - 2, 1), (NP - 1, 1)]
NG = len(GROUPS)
XCH = [(0, 2), (2, 2), (4, 4)] + [(t, 8) for t in range(8, NT, 8)]
FG, IG, OG, UG = 0, 1, 2, 3
TAGS = ["F", "I", "O", "U"]


def chunk_of(t):
    for ci, (t0, n) in enumerate(XCH):
        if t0 <= t < t0 + n:
            return ci, t - t0
    raise ValueError("tile outside the table")


def group_of(k):
    for g, (k0, n) in enumerate(GROUPS):
        if k0 <= k < k0 + n:
            return g, k - k0
    raise ValueError("pair outside the table")


def tile_lstmhardcell_t_kernel(tc, x, state, cell, W_in, W_h, out_0, out_1):
    nc = tc.nc
    with ExitStack() as ctx:
        const = ctx.enter_context(tc.tile_pool(name="const", bufs=1))
        inp = ctx.enter_context(tc.tile_pool(name="inp", bufs=1))
        wpool = ctx.enter_context(tc.tile_pool(name="wpool", bufs=1))
        zpool = ctx.enter_context(tc.tile_pool(name="zpool", bufs=4))
        work = ctx.enter_context(tc.tile_pool(name="work", bufs=2))
        psum = ctx.enter_context(tc.psum_pool(name="psum", bufs=1))
        if MANUAL:
            ctx.enter_context(tc.manual_schedule())

        xv = x.rearrange("(p t) k -> p (t k)", t=NT)
        sv = state.rearrange("(p t) k -> p (t k)", t=NT)
        cv = cell.rearrange("(p t) k -> p (t k)", t=NT)
        o0v = out_0.rearrange("(p t) h -> p (t h)", t=NT)
        o1v = out_1.rearrange("(p t) h -> p (t h)", t=NT)
        wiv = W_in.rearrange("n h k -> (n h) k").rearrange("(a p) k -> p a k", p=P)
        whv = W_h.rearrange("n h k -> (n h) k").rearrange("(a p) k -> p a k", p=P)

        xs, ss, cs = {}, {}, {}
        win, wh = {}, {}

        def load_z(ci):
            t0, n = XCH[ci]
            xs[ci] = inp.tile([P, n * I], BF16, name="x%d" % ci)
            nc.sync.dma_start(out=xs[ci][:], in_=xv[:, t0 * I:(t0 + n) * I])
            ss[ci] = inp.tile([P, n * H], BF16, name="s%d" % ci)
            nc.sync.dma_start(out=ss[ci][:], in_=sv[:, t0 * H:(t0 + n) * H])

        def load_c(ci):
            t0, n = XCH[ci]
            cs[ci] = inp.tile([P, n * H], BF16, name="c%d" % ci)
            nc.sync.dma_start(out=cs[ci][:], in_=cv[:, t0 * H:(t0 + n) * H])

        def load_w(n):
            win[n] = wpool.tile([P, 2 * I], BF16, name="win%d" % n)
            nc.sync.dma_start(out=win[n][:].rearrange("p (a k) -> p a k", a=2),
                              in_=wiv[:, 2 * n:2 * n + 2, :])
            wh[n] = wpool.tile([P, 2 * H], BF16, name="wh%d" % n)
            nc.sync.dma_start(out=wh[n][:].rearrange("p (a k) -> p a k", a=2),
                              in_=whv[:, 2 * n:2 * n + 2, :])

        loads = []
        for ci, (t0, n) in enumerate(XCH):
            loads.append((t0 // 2 - LEAD_T, 0, load_z, ci))
            loads.append((t0 // 2, 1, load_c, ci))
        loads = [e for e in sorted(loads, key=lambda e: (e[0], e[1])) if e[3] > 0]
        done = [0]

        def emit_loads(s):
            while done[0] < len(loads) and loads[done[0]][0] - MARGIN <= s:
                e = loads[done[0]]
                done[0] += 1
                e[2](e[3])

        load_w(FG)
        load_z(0)
        load_w(UG)
        load_c(0)
        load_w(IG)
        load_w(OG)
        emit_loads(-LEAD_T)

        ident_f = const.tile([P, P], F32, name="ident_f")
        make_identity(nc, ident_f[:])
        warm = const.tile([P, 8], F32, name="warm")
        nc.vector.memset(warm[:], 0.0)
        nc.scalar.activation(out=warm[:], in_=warm[:], func=ACTF.Sigmoid)

        TB, GRP, ZC, ZS, BK = {}, {}, {}, {}, {}
        SG = {}
        US, T4 = {}, {}
        wc, ws = {}, {}
        copied = set()
        quantised = set()

        def ok(k):
            return 0 <= k < NP

        def tr(k):
            TB[k] = psum.tile([P, 512], F32, name="tb", tag="T", bufs=2)
            for u, src in enumerate((xs, ss)):
                for t in range(2):
                    ci, off = chunk_of(2 * k + t)
                    v = src[ci][:].bitcast(F32)
                    nc.tensor.transpose(TB[k][:, u * 256 + t * P:u * 256 + (t + 1) * P],
                                        v[:, off * P:(off + 1) * P], ident_f[:])

        def interleave(eng_copy, dst_f32, bank):
            eng_copy(out=dst_f32.rearrange("p (c u) -> p c u", u=2),
                     in_=bank[:].rearrange("p (u c) -> p c u", u=2))

        def ev(k):
            g, pos = group_of(k)
            if pos == 0:
                GRP[g] = zpool.tile([P, 2048], BF16, name="grp", tag="grp", align_bytes=64)
            interleave(nc.scalar.copy, GRP[g][:].bitcast(F32)[:, pos * 512:(pos + 1) * 512], TB[k])
            copied.add(k)

        def qz(g):
            n = GROUPS[g][1]
            ZC[g] = zpool.tile([P, 512], U32, name="zc", tag="zc", align_bytes=64)
            ZS[g] = zpool.tile([P, 512], U8, name="zs", tag="zs", align_bytes=64)
            nc.vector.quantize_mx(out=ZC[g][:, :n * 256].bitcast(FP8X4), scales=ZS[g][:, :n * 256],
                                  in_=GRP[g][:, :n * 1024])
            quantised.add(g)

        def mx(k, n):
            g, pos = group_of(k)
            BK[(n, k)] = psum.tile([P, 512], F32, name="bk" + TAGS[n], tag=TAGS[n], bufs=2 if n == UG else 1)
            for t in range(2):
                c0 = (2 * pos + t) * P
                nc.tensor.matmul_mx(out=BK[(n, k)][:, t * H:(t + 1) * H],
                                    lhsT=ZC[g][:, c0:c0 + P].bitcast(FP8X4),
                                    lhsT_scale=ZS[g][:, c0:c0 + P],
                                    rhs=wc[n][:].bitcast(FP8X4),
                                    rhs_scale=ws[n][:],
                                    start=True, stop=True)

        def act(k, n):
            g, pos = group_of(k)
            if pos == 0:
                SG[(n, g)] = work.tile([P, 1024], F32, name="sg" + TAGS[n], tag="sg" + TAGS[n],
                                       bufs=4 if n in (FG, OG) else 3)
            dst = SG[(n, g)][:, pos * 512:(pos + 1) * 512]
            if n == UG and rr(g):
                nc.scalar.activation(out=dst, in_=BK[(n, k)][:], func=ACTF.Relu, bias=1.0, scale=-1.0)
                if pos == GROUPS[g][1] - 1:
                    whole = SG[(n, g)][:, :cols(g)]
                    nc.scalar.activation(out=whole, in_=whole, func=ACTF.Relu, bias=2.0, scale=-1.0)
            elif n == UG:
                nc.scalar.activation(out=dst, in_=BK[(n, k)][:], func=ACTF.Relu, bias=1.0)
            else:
                nc.scalar.activation(out=dst, in_=BK[(n, k)][:], func=ACTF.Sigmoid)

        def w_gate(n, eng_copy):
            wb = psum.tile([P, 512], F32, name="wb", tag=TAGS[n], bufs=2 if n == UG else 1)
            for u, src in enumerate((win, wh)):
                v = src[n][:].bitcast(F32)
                for r in range(2):
                    nc.tensor.transpose(wb[:, u * 256 + r * P:u * 256 + (r + 1) * P],
                                        v[:, r * P:(r + 1) * P], ident_f[:])
            wg = wpool.tile([P, 1024], BF16, name="wg%d" % n, align_bytes=64)
            interleave(eng_copy, wg[:].bitcast(F32), wb)
            wc[n] = wpool.tile([P, 256], U32, name="wc%d" % n, align_bytes=64)
            ws[n] = wpool.tile([P, 256], U8, name="ws%d" % n, align_bytes=64)
            nc.vector.quantize_mx(out=wc[n][:].bitcast(FP8X4), scales=ws[n][:], in_=wg[:])

        def rr(g):
            return g in RR_SET

        def cols(g):
            return GROUPS[g][1] * 512

        def dram_cols(g):
            k0, n = GROUPS[g]
            return slice(2 * k0 * H, 2 * (k0 + n) * H)

        def clip_u(g):
            w = cols(g)
            US[g] = work.tile([P, 1024], F32, name="us", tag="us")
            if g < D_UNTIL:
                for j in range(GROUPS[g][1]):
                    nc.vector.tensor_scalar(out=US[g][:, j * 512:(j + 1) * 512], in0=BK[(UG, GROUPS[g][0] + j)][:],
                                            scalar1=-1.0, scalar2=1.0, op0=ALU.max, op1=ALU.min)
                return
            nc.vector.tensor_scalar(out=US[g][:, :w], in0=SG[(UG, g)][:, :w], scalar1=2.0, scalar2=-1.0,
                                    op0=ALU.min, op1=ALU.add)

        def f_cell(g):
            w = cols(g)
            ci, off = chunk_of(2 * GROUPS[g][0])
            f = SG[(FG, g)][:, :w]
            nc.vector.tensor_tensor(out=f, in0=f, in1=cs[ci][:, off * H:off * H + w], op=ALU.mult)

        def i_u(g):
            w = cols(g)
            if rr(g):
                US[g] = work.tile([P, 1024], F32, name="us", tag="us")
                nc.vector.scalar_tensor_tensor(out=US[g][:, :w], in0=SG[(UG, g)][:, :w], scalar=-1.0,
                                               in1=SG[(IG, g)][:, :w], op0=ALU.add, op1=ALU.mult)
                return
            nc.vector.tensor_tensor(out=US[g][:, :w], in0=SG[(IG, g)][:, :w], in1=US[g][:, :w], op=ALU.mult)

        def new_cell(g):
            w = cols(g)
            f = SG[(FG, g)][:, :w]
            nc.vector.tensor_tensor(out=f, in0=f, in1=US[g][:, :w], op=ALU.add)
            nc.sync.dma_start(out=o1v[:, dram_cols(g)], in_=f)

        def clip_c(g):
            w = cols(g)
            T4[g] = work.tile([P, 1024], F32, name="t4", tag="t4")
            nc.vector.tensor_scalar(out=T4[g][:, :w], in0=SG[(FG, g)][:, :w], scalar1=-1.0, scalar2=1.0,
                                    op0=ALU.max, op1=ALU.min)

        def new_state(g):
            w = cols(g)
            o = SG[(OG, g)][:, :w]
            nc.vector.tensor_tensor(out=o, in0=o, in1=T4[g][:, :w], op=ALU.mult)
            nc.sync.dma_start(out=o0v[:, dram_cols(g)], in_=o)

        def ready(g):
            k0, n = GROUPS[g]
            return all((k0 + j) in copied for j in range(n))

        w_gate(FG, nc.scalar.copy)
        tr(0)
        ev(0)
        qz(0)
        w_gate(UG, nc.scalar.copy)
        w_gate(IG, nc.vector.tensor_copy)
        w_gate(OG, nc.vector.tensor_copy)
        nxt = [1]
        order = (FG, UG, IG, OG)
        for s in range(-LEAD_S, NP):
            emit_loads(s)
            if ok(s) and group_of(s)[1] == GROUPS[group_of(s)[0]][1] - 1:
                g = group_of(s)[0]
                f_cell(g)
                if g > 0:
                    clip_c(g - 1)
                if not rr(g):
                    clip_u(g)
                else:
                    i_u(g)
                if g > 0:
                    new_state(g - 1)
                if not rr(g):
                    i_u(g)
                if g + 2 < NG and (g + 2) not in quantised and ready(g + 2):
                    qz(g + 2)
                new_cell(g)
            k = s + LEAD_S
            if ok(k):
                if group_of(k)[0] not in quantised:
                    qz(group_of(k)[0])
                for n in order:
                    mx(k, n)
            first = nxt[0]
            while nxt[0] <= min(s + LEAD_T, NP - 1) and nxt[0] - first < 2:
                tr(nxt[0])
                nxt[0] += 1
            if ok(k):
                for n in order:
                    if n != UG or group_of(k)[0] >= D_UNTIL:
                        act(k, n)
            for j in range(first, nxt[0]):
                ev(j)
        clip_c(NG - 1)
        new_state(NG - 1)
